import numpy as np
import ml_dtypes


def mxq(x, axis, fmt="e4m3"):
    dtype, down = {"e4m3": (ml_dtypes.float8_e4m3fn, 7), "e5m2": (ml_dtypes.float8_e5m2, 14)}[fmt]
    v = np.moveaxis(np.asarray(x, np.float32).astype(ml_dtypes.bfloat16).astype(np.float64), axis, -1)
    blocks = v.reshape(v.shape[:-1] + (-1, 32))
    amax = np.abs(blocks).max(-1, keepdims=True)
    byte = np.maximum(np.where(amax > 0, np.frexp(amax)[1] - 1 + 127, 0) - down, 1)
    scale = np.exp2(byte - 127.0)
    codes = (blocks / scale).astype(np.float32).astype(dtype).astype(np.float64)
    return np.moveaxis((codes * scale).reshape(v.shape), -1, axis)


WIDE = False


def mx_kscale(k):
    if not WIDE:
        return np.ones(k)
    levels = np.array([10, -10, 5, -5, 0])
    a = np.random.permutation(np.resize(levels, k // 512 * 4)).reshape(k // 512, 4)
    idx = np.arange(k)
    return np.exp2(a[idx // 512, idx % 128 // 32])


BF16 = ml_dtypes.bfloat16


def bf(x):
    return np.asarray(x, np.float32).astype(BF16)


def f64(x):
    return np.asarray(x).astype(np.float64)


E2M1 = np.array([0.0, 0.5, 1.0, 1.5, 2.0, 3.0, 4.0, 6.0, -0.0, -0.5, -1.0, -1.5, -2.0, -3.0, -4.0, -6.0])


def pack_weight(w, fmt):
    k, n = w.shape
    w = f64(bf(w)).reshape(k // 32, 32, n)
    amax = np.abs(w).max(1)
    if fmt == "e4m3":
        byte = np.frexp(amax)[1] - 1 + 127 - 7
    else:
        mant, ex = np.frexp(amax / 6.0)
        byte = np.where(mant > 0.5, ex, ex - 1) + 127
    byte = np.clip(np.where(amax > 0, byte, 1), 1, 254)
    scaled = (w * np.exp2(127.0 - byte)[:, None, :]).reshape(k, n).astype(np.float32)
    by_word = np.ascontiguousarray(scaled.reshape(k // 512, 128, 4, n).transpose(0, 1, 3, 2))
    if fmt == "e4m3":
        words = by_word.astype(ml_dtypes.float8_e4m3fn).view(np.uint8)
    else:
        c = by_word.astype(ml_dtypes.float4_e2m1fn).view(np.uint8) & 0xF
        words = c[..., 0::2] | (c[..., 1::2] << 4)
    return np.ascontiguousarray(words), np.ascontiguousarray(byte.astype(np.uint8).reshape(k // 512, 16, n))


def unpack_weight(words, scales, fmt):
    g, p, n, _ = words.shape
    if fmt == "e4m3":
        vals = np.ascontiguousarray(words).view(ml_dtypes.float8_e4m3fn).astype(np.float64)
    else:
        nib = np.empty((g, p, n, 4), np.uint8)
        nib[..., 0::2] = words & 0xF
        nib[..., 1::2] = words >> 4
        vals = E2M1[nib]
    vals = vals * np.repeat(np.exp2(scales.astype(np.float64) - 127.0), 8, axis=1)[..., None]
    return vals.transpose(0, 1, 3, 2).reshape(g * 512, n)


B, D_IN, H = 512, 512, 1024


def sigmoid(v):
    return 1.0 / (1.0 + np.exp(-v))


def setup_inputs():
    s, u, v = mx_kscale(D_IN), mx_kscale(H), mx_kscale(H)
    one = np.ones(H)
    inp = {"x": bf(np.random.standard_normal((B, D_IN)) * s),
           "hidden_memory_tm1": bf(np.random.standard_normal((B, 2 * H)) * np.concatenate([u, one])),
           "hidden_memory_tm2": bf(np.random.standard_normal((B, 2 * H)) * np.concatenate([v, one]))}
    for g in "ifoc":
        inp["W" + g + "_words"], inp["W" + g + "_scales"] = pack_weight(np.random.standard_normal((D_IN, H)) * 0.6 / np.sqrt(D_IN) / s[:, None], "e4m3")
        inp["U" + g + "_words"], inp["U" + g + "_scales"] = pack_weight(np.random.standard_normal((H, H)) * 0.6 / np.sqrt(H) / u[:, None], "e4m3")
        inp["V" + g + "_words"], inp["V" + g + "_scales"] = pack_weight(np.random.standard_normal((H, H)) * 0.6 / np.sqrt(H) / v[:, None], "e4m3")
    return inp


def reference(x, hidden_memory_tm1, hidden_memory_tm2, Wi_words, Wi_scales, Ui_words, Ui_scales, Vi_words, Vi_scales, Wf_words, Wf_scales, Uf_words, Uf_scales, Vf_words, Vf_scales, Wo_words, Wo_scales, Uo_words, Uo_scales, Vo_words, Vo_scales, Wc_words, Wc_scales, Uc_words, Uc_scales, Vc_words, Vc_scales):
    hm1 = f64(hidden_memory_tm1)
    hm2 = f64(hidden_memory_tm2)
    h_prev = hm1[:, :H]
    c_prev = hm1[:, H:]
    h_cross = hm2[:, :H]
    W = np.concatenate([unpack_weight(Wi_words, Wi_scales, "e4m3"), unpack_weight(Wf_words, Wf_scales, "e4m3"), unpack_weight(Wo_words, Wo_scales, "e4m3"), unpack_weight(Wc_words, Wc_scales, "e4m3")], axis=1)
    U = np.concatenate([unpack_weight(Ui_words, Ui_scales, "e4m3"), unpack_weight(Uf_words, Uf_scales, "e4m3"), unpack_weight(Uo_words, Uo_scales, "e4m3"), unpack_weight(Uc_words, Uc_scales, "e4m3")], axis=1)
    V = np.concatenate([unpack_weight(Vi_words, Vi_scales, "e4m3"), unpack_weight(Vf_words, Vf_scales, "e4m3"), unpack_weight(Vo_words, Vo_scales, "e4m3"), unpack_weight(Vc_words, Vc_scales, "e4m3")], axis=1)
    gates = ((mxq(f64(x), 1, "e4m3") @ W)
             + (mxq(h_prev, 1, "e4m3") @ U)
             + (mxq(h_cross, 1, "e4m3") @ V))
    i = sigmoid(gates[:, 0 * H:1 * H])
    f = sigmoid(gates[:, 1 * H:2 * H])
    o = sigmoid(gates[:, 2 * H:3 * H])
    c_ = np.tanh(gates[:, 3 * H:4 * H])
    c = f * c_prev + i * c_
    h = o * np.tanh(c)
    new_state = np.concatenate([h, c], axis=-1)
    return h, new_state

@@ -1,0 +1,257 @@
+from contextlib import ExitStack
+
+import concourse.mybir as mybir
+from concourse.masks import make_identity
+
+F32 = mybir.dt.float32
+BF16 = mybir.dt.bfloat16
+I32 = mybir.dt.int32
+U32 = mybir.dt.uint32
+U8 = mybir.dt.uint8
+FP8X4 = mybir.dt.float8_e4m3fn_x4
+ACT = mybir.ActivationFunctionType
+
+P = 128
+PACK = 4
+K_PASS = P * PACK
+WORDS_PASS = K_PASS // 2
+QUADRANTS = 4
+LIVE_ROWS = 4
+
+BATCH, D_IN, HID = 512, 512, 1024
+ROW_TILES = BATCH // P
+N_TILE = 512
+CHUNKS = HID // N_TILE
+
+GATES_AS_GIVEN = "ifoc"
+GATE_ORDER = "icfo"
+MATRICES = "WUV"
+PASSES = {"W": D_IN // K_PASS, "U": HID // K_PASS, "V": HID // K_PASS}
+
+K_TOTAL = D_IN + 2 * HID
+FLOPS = 2 * BATCH * K_TOTAL * 4 * HID
+BYTES = (
+    2 * BATCH * (D_IN + 3 * HID)
+    + K_TOTAL * 4 * HID
+    + K_TOTAL * 4 * HID // 32
+    + 4 * BATCH * 3 * HID
+)
+
+
+def tile_bilaterallstmcell_kernel(
+    tc, x, hidden_memory_tm1, hidden_memory_tm2, *weights_and_outputs
+):
+    nc = tc.nc
+    out_h, out_state = weights_and_outputs[24:]
+    dram_words = {}
+    dram_scales = {}
+    for gate_index, gate in enumerate(GATES_AS_GIVEN):
+        for matrix_index, matrix in enumerate(MATRICES):
+            first = 2 * (len(MATRICES) * gate_index + matrix_index)
+            dram_words[gate, matrix] = weights_and_outputs[first]
+            dram_scales[gate, matrix] = weights_and_outputs[first + 1]
+    operand = {
+        "W": x,
+        "U": hidden_memory_tm1[:, 0:HID],
+        "V": hidden_memory_tm2[:, 0:HID],
+    }
+
+    with ExitStack() as ctx:
+        ctx.enter_context(tc.manual_schedule())
+        keep = ctx.enter_context(tc.tile_pool(name="keep", bufs=1))
+        stage = ctx.enter_context(tc.tile_pool(name="stage", bufs=4))
+        gates = ctx.enter_context(tc.tile_pool(name="gates", bufs=ROW_TILES))
+        outs = ctx.enter_context(tc.tile_pool(name="outs", bufs=ROW_TILES * CHUNKS))
+        psum = ctx.enter_context(tc.psum_pool(name="psum", bufs=ROW_TILES))
+
+        identity = keep.tile([P, P], F32, name="identity")
+        make_identity(nc, identity[:])
+        warm = keep.tile([P, 1], F32, name="warm")
+        nc.vector.memset(warm[:], 0.0)
+        nc.scalar.activation(out=warm[:], in_=warm[:], func=ACT.Sigmoid)
+
+        weight_planes = {}
+        for gate in GATE_ORDER:
+            for matrix in MATRICES:
+                plane = keep.tile(
+                    [P, HID], U8, name="plane_%s%s" % (matrix, gate), align_bytes=64
+                )
+                nc.vector.memset(plane[:].bitcast(I32), 0)
+                weight_planes[gate, matrix] = plane
+
+        raw = {}
+        weight_words = {}
+
+        def load_operand(matrix):
+            width = PASSES[matrix] * K_PASS
+            for m in range(ROW_TILES):
+                rows = keep.tile([P, width], BF16, name="raw_%s%d" % (matrix, m))
+                nc.sync.dma_start(out=rows[:], in_=operand[matrix][m * P : (m + 1) * P, :])
+                raw[matrix, m] = rows
+
+        def load_scales(gate, matrix):
+            passes = PASSES[matrix]
+            plane = weight_planes[gate, matrix]
+            for quadrant in range(QUADRANTS):
+                first = 32 * quadrant
+                rows = slice(LIVE_ROWS * quadrant, LIVE_ROWS * (quadrant + 1))
+                nc.sync.dma_start(
+                    out=plane[first : first + LIVE_ROWS * passes, :].bitcast(I32),
+                    in_=dram_scales[gate, matrix][:, rows, :].bitcast(I32),
+                )
+
+        def load_words(gate, matrix, chunk):
+            for g in range(PASSES[matrix]):
+                words = keep.tile(
+                    [P, N_TILE],
+                    U32,
+                    name="words_%s%s%d_%d" % (matrix, gate, g, chunk),
+                    align_bytes=64,
+                )
+                source = dram_words[gate, matrix][g].rearrange("p n t -> p (n t)").bitcast(I32)
+                nc.sync.dma_start(
+                    out=words[:].bitcast(I32),
+                    in_=source[:, chunk * N_TILE : (chunk + 1) * N_TILE],
+                )
+                weight_words[gate, matrix, g, chunk] = words
+
+        c_prev = {}
+
+        def load_c_prev(chunk):
+            first = HID + chunk * N_TILE
+            tile_c = keep.tile([P, ROW_TILES, N_TILE], BF16, name="c_prev%d" % chunk)
+            nc.sync.dma_start(
+                out=tile_c[:],
+                in_=hidden_memory_tm1[:, first : first + N_TILE].rearrange(
+                    "(m p) n -> p m n", p=P
+                ),
+            )
+            c_prev[chunk] = tile_c
+
+        for chunk in range(CHUNKS):
+            for gate in GATE_ORDER:
+                for matrix in MATRICES:
+                    if chunk == 0:
+                        if gate == GATE_ORDER[0]:
+                            load_operand(matrix)
+                        load_scales(gate, matrix)
+                    load_words(gate, matrix, chunk)
+                if gate == "f":
+                    load_c_prev(chunk)
+
+        codes = {}
+        code_planes = {}
+
+        def quantise_rows(matrix, m):
+            passes = PASSES[matrix]
+            raw_words = raw[matrix, m][:].bitcast(F32)
+            flipped = psum.tile([P, N_TILE], F32, name="flipped", tag="odd")
+            for g in range(passes):
+                for u in range(2):
+                    slot = 2 * g + u
+                    nc.tensor.transpose(
+                        out=flipped[:, slot * P : (slot + 1) * P],
+                        in_=raw_words[:, WORDS_PASS * g + u : WORDS_PASS * (g + 1) : 2],
+                        identity=identity[:],
+                    )
+            grouped = stage.tile(
+                [P, passes * P * PACK], BF16, name="grouped", tag="grouped", align_bytes=64
+            )
+            nc.scalar.copy(
+                out=grouped[:].bitcast(F32).rearrange("p (g r u) -> p g r u", g=passes, u=2),
+                in_=flipped[:, 0 : passes * 2 * P].rearrange(
+                    "p (g u r) -> p g r u", g=passes, u=2
+                ),
+            )
+            packed = keep.tile(
+                [P, passes * P], U32, name="codes_%s%d" % (matrix, m), align_bytes=64
+            )
+            plane = keep.tile(
+                [P, passes * P], U8, name="code_plane_%s%d" % (matrix, m), align_bytes=64
+            )
+            nc.vector.quantize_mx(out=packed[:].bitcast(FP8X4), scales=plane[:], in_=grouped[:])
+            codes[matrix, m] = packed
+            code_planes[matrix, m] = plane
+
+        def mx_pass(bank, gate, matrix, g, chunk, m):
+            rows = slice(g * P, (g + 1) * P)
+            nc.tensor.matmul_mx(
+                out=bank[:],
+                lhsT=codes[matrix, m][:, rows].bitcast(FP8X4),
+                lhsT_scale=code_planes[matrix, m][:, rows],
+                rhs=weight_words[gate, matrix, g, chunk][:].bitcast(FP8X4),
+                rhs_scale=weight_planes[gate, matrix][
+                    LIVE_ROWS * g : P, chunk * N_TILE : (chunk + 1) * N_TILE
+                ],
+                start=(matrix == MATRICES[0]),
+                stop=(matrix == MATRICES[-1] and g == PASSES[matrix] - 1),
+            )
+
+        value = {}
+
+        def after_gate(gate, chunk, banks, row_tiles):
+            cols = slice(chunk * N_TILE, (chunk + 1) * N_TILE)
+            for m in row_tiles:
+                value[gate, m] = gates.tile([P, N_TILE], F32, name="gate_" + gate, tag=gate)
+                nc.scalar.activation(
+                    out=value[gate, m][:],
+                    in_=banks[m][:],
+                    func=(ACT.Tanh if gate == "c" else ACT.Sigmoid),
+                )
+            if gate == "c":
+                for m in row_tiles:
+                    nc.vector.tensor_mul(
+                        out=value["i", m][:], in0=value["i", m][:], in1=value["c", m][:]
+                    )
+            if gate == "f":
+                for m in row_tiles:
+                    rows = slice(m * P, (m + 1) * P)
+                    nc.vector.tensor_mul(
+                        out=value["f", m][:], in0=value["f", m][:], in1=c_prev[chunk][:, m, :]
+                    )
+                    value["new_c", m] = outs.tile([P, N_TILE], F32, name="new_c", tag="new_c")
+                    nc.vector.tensor_add(
+                        out=value["new_c", m][:], in0=value["f", m][:], in1=value["i", m][:]
+                    )
+                    nc.sync.dma_start(
+                        out=out_state[rows, HID + chunk * N_TILE : HID + (chunk + 1) * N_TILE],
+                        in_=value["new_c", m][:],
+                    )
+                for m in row_tiles:
+                    value["tanh_c", m] = gates.tile([P, N_TILE], F32, name="tanh_c", tag="tanh_c")
+                    nc.scalar.activation(
+                        out=value["tanh_c", m][:], in_=value["new_c", m][:], func=ACT.Tanh
+                    )
+            if gate == "o":
+                for m in row_tiles:
+                    rows = slice(m * P, (m + 1) * P)
+                    new_h = outs.tile([P, N_TILE], F32, name="new_h", tag="new_h")
+                    nc.vector.tensor_mul(
+                        out=new_h[:], in0=value["o", m][:], in1=value["tanh_c", m][:]
+                    )
+                    nc.sync.dma_start(out=out_h[rows, cols], in_=new_h[:])
+                    nc.sync.dma_start(out=out_state[rows, cols], in_=new_h[:])
+
+        for chunk in range(CHUNKS):
+            for gate_index, gate in enumerate(GATE_ORDER):
+                banks = [
+                    psum.tile(
+                        [P, N_TILE], F32, name="sum%d" % m, tag=("even", "odd")[gate_index % 2]
+                    )
+                    for m in range(ROW_TILES)
+                ]
+                if chunk == CHUNKS - 1 and gate == GATE_ORDER[-1]:
+                    for m in range(ROW_TILES):
+                        for matrix in MATRICES:
+                            for g in range(PASSES[matrix]):
+                                mx_pass(banks[m], gate, matrix, g, chunk, m)
+                        after_gate(gate, chunk, banks, [m])
+                else:
+                    for matrix in MATRICES:
+                        if chunk == 0 and gate_index == 0:
+                            for m in range(ROW_TILES):
+                                quantise_rows(matrix, m)
+                        for g in range(PASSES[matrix]):
+                            for m in range(ROW_TILES):
+                                mx_pass(banks[m], gate, matrix, g, chunk, m)
+                    after_gate(gate, chunk, banks, range(ROW_TILES))

@@ -95,25 +95,25 @@ def tile_bilaterallstmcell_kernel(
             for quadrant in range(QUADRANTS):
                 first = 32 * quadrant
                 rows = slice(LIVE_ROWS * quadrant, LIVE_ROWS * (quadrant + 1))
-                nc.sync.dma_start(
-                    out=plane[first : first + LIVE_ROWS * passes, :].bitcast(I32),
-                    in_=dram_scales[gate, matrix][:, rows, :].bitcast(I32),
+                queue, word = (nc.sync, I32) if quadrant % 2 == 0 else (nc.gpsimd, F32)
+                queue.dma_start(
+                    out=plane[first : first + LIVE_ROWS * passes, :].bitcast(word),
+                    in_=dram_scales[gate, matrix][:, rows, :].bitcast(word),
                 )
 
         def load_words(gate, matrix, chunk):
-            for g in range(PASSES[matrix]):
-                words = keep.tile(
-                    [P, N_TILE],
-                    U32,
-                    name="words_%s%s%d_%d" % (matrix, gate, g, chunk),
-                    align_bytes=64,
-                )
-                source = dram_words[gate, matrix][g].rearrange("p n t -> p (n t)").bitcast(I32)
-                nc.sync.dma_start(
-                    out=words[:].bitcast(I32),
-                    in_=source[:, chunk * N_TILE : (chunk + 1) * N_TILE],
-                )
-                weight_words[gate, matrix, g, chunk] = words
+            words = keep.tile(
+                [P, PASSES[matrix], N_TILE],
+                U32,
+                name="words_%s%s_%d" % (matrix, gate, chunk),
+                align_bytes=64,
+            )
+            source = dram_words[gate, matrix].rearrange("g p n t -> p g (n t)").bitcast(I32)
+            nc.sync.dma_start(
+                out=words[:].bitcast(I32),
+                in_=source[:, :, chunk * N_TILE : (chunk + 1) * N_TILE],
+            )
+            weight_words[gate, matrix, chunk] = words
 
         c_prev = {}
 
@@ -179,7 +179,7 @@ def tile_bilaterallstmcell_kernel(
                 out=bank[:],
                 lhsT=codes[matrix, m][:, rows].bitcast(FP8X4),
                 lhsT_scale=code_planes[matrix, m][:, rows],
-                rhs=weight_words[gate, matrix, g, chunk][:].bitcast(FP8X4),
+                rhs=weight_words[gate, matrix, chunk][:, g, :].bitcast(FP8X4),
                 rhs_scale=weight_planes[gate, matrix][
                     LIVE_ROWS * g : P, chunk * N_TILE : (chunk + 1) * N_TILE
                 ],
@@ -191,6 +191,12 @@ def tile_bilaterallstmcell_kernel(
 
         def after_gate(gate, chunk, banks, row_tiles):
             cols = slice(chunk * N_TILE, (chunk + 1) * N_TILE)
+            if gate == "o":
+                for m in row_tiles:
+                    value["tanh_c", m] = gates.tile([P, N_TILE], F32, name="tanh_c", tag="tanh_c")
+                    nc.scalar.activation(
+                        out=value["tanh_c", m][:], in_=value["new_c", m][:], func=ACT.Tanh
+                    )
             for m in row_tiles:
                 value[gate, m] = gates.tile([P, N_TILE], F32, name="gate_" + gate, tag=gate)
                 nc.scalar.activation(
@@ -217,11 +223,6 @@ def tile_bilaterallstmcell_kernel(
                         out=out_state[rows, HID + chunk * N_TILE : HID + (chunk + 1) * N_TILE],
                         in_=value["new_c", m][:],
                     )
-                for m in row_tiles:
-                    value["tanh_c", m] = gates.tile([P, N_TILE], F32, name="tanh_c", tag="tanh_c")
-                    nc.scalar.activation(
-                        out=value["tanh_c", m][:], in_=value["new_c", m][:], func=ACT.Tanh
-                    )
             if gate == "o":
                 for m in row_tiles:
                     rows = slice(m * P, (m + 1) * P)
@@ -240,7 +241,7 @@ def tile_bilaterallstmcell_kernel(
                     )
                     for m in range(ROW_TILES)
                 ]
-                if chunk == CHUNKS - 1 and gate == GATE_ORDER[-1]:
+                if chunk == CHUNKS - 1 and gate in GATE_ORDER[-2:]:
                     for m in range(ROW_TILES):
                         for matrix in MATRICES:
                             for g in range(PASSES[matrix]):

@@ -95,10 +95,9 @@ def tile_bilaterallstmcell_kernel(
             for quadrant in range(QUADRANTS):
                 first = 32 * quadrant
                 rows = slice(LIVE_ROWS * quadrant, LIVE_ROWS * (quadrant + 1))
-                queue, word = (nc.sync, I32) if quadrant % 2 == 0 else (nc.gpsimd, F32)
-                queue.dma_start(
-                    out=plane[first : first + LIVE_ROWS * passes, :].bitcast(word),
-                    in_=dram_scales[gate, matrix][:, rows, :].bitcast(word),
+                nc.sync.dma_start(
+                    out=plane[first : first + LIVE_ROWS * passes, :].bitcast(I32),
+                    in_=dram_scales[gate, matrix][:, rows, :].bitcast(I32),
                 )
 
         def load_words(gate, matrix, chunk):

@@ -60,8 +60,8 @@ def tile_bilaterallstmcell_kernel(
         ctx.enter_context(tc.manual_schedule())
         keep = ctx.enter_context(tc.tile_pool(name="keep", bufs=1))
         stage = ctx.enter_context(tc.tile_pool(name="stage", bufs=4))
-        gates = ctx.enter_context(tc.tile_pool(name="gates", bufs=ROW_TILES))
-        outs = ctx.enter_context(tc.tile_pool(name="outs", bufs=ROW_TILES * CHUNKS))
+        brief = ctx.enter_context(tc.tile_pool(name="brief", bufs=ROW_TILES))
+        lasting = ctx.enter_context(tc.tile_pool(name="lasting", bufs=ROW_TILES * CHUNKS))
         psum = ctx.enter_context(tc.psum_pool(name="psum", bufs=ROW_TILES))
 
         identity = keep.tile([P, P], F32, name="identity")
@@ -127,8 +127,8 @@ def tile_bilaterallstmcell_kernel(
             )
             c_prev[chunk] = tile_c
 
-        for chunk in range(CHUNKS):
-            for gate in GATE_ORDER:
+        for gate in GATE_ORDER:
+            for chunk in range(CHUNKS):
                 for matrix in MATRICES:
                     if chunk == 0:
                         if gate == GATE_ORDER[0]:
@@ -188,70 +188,80 @@ def tile_bilaterallstmcell_kernel(
 
         value = {}
 
-        def after_gate(gate, chunk, banks, row_tiles):
+        def after_passes(gate, chunk, banks, row_tiles):
             cols = slice(chunk * N_TILE, (chunk + 1) * N_TILE)
             if gate == "o":
                 for m in row_tiles:
-                    value["tanh_c", m] = gates.tile([P, N_TILE], F32, name="tanh_c", tag="tanh_c")
+                    value["tanh_c", chunk, m] = brief.tile(
+                        [P, N_TILE], F32, name="tanh_c", tag="tanh_c"
+                    )
                     nc.scalar.activation(
-                        out=value["tanh_c", m][:], in_=value["new_c", m][:], func=ACT.Tanh
+                        out=value["tanh_c", chunk, m][:],
+                        in_=value["new_c", chunk, m][:],
+                        func=ACT.Tanh,
                     )
             for m in row_tiles:
-                value[gate, m] = gates.tile([P, N_TILE], F32, name="gate_" + gate, tag=gate)
+                pool = lasting if gate == "i" else brief
+                value[gate, chunk, m] = pool.tile([P, N_TILE], F32, name="gate_" + gate, tag=gate)
                 nc.scalar.activation(
-                    out=value[gate, m][:],
+                    out=value[gate, chunk, m][:],
                     in_=banks[m][:],
                     func=(ACT.Tanh if gate == "c" else ACT.Sigmoid),
                 )
             if gate == "c":
                 for m in row_tiles:
                     nc.vector.tensor_mul(
-                        out=value["i", m][:], in0=value["i", m][:], in1=value["c", m][:]
+                        out=value["i", chunk, m][:],
+                        in0=value["i", chunk, m][:],
+                        in1=value["c", chunk, m][:],
                     )
             if gate == "f":
                 for m in row_tiles:
-                    rows = slice(m * P, (m + 1) * P)
                     nc.vector.tensor_mul(
-                        out=value["f", m][:], in0=value["f", m][:], in1=c_prev[chunk][:, m, :]
+                        out=value["f", chunk, m][:],
+                        in0=value["f", chunk, m][:],
+                        in1=c_prev[chunk][:, m, :],
                     )
-                    value["new_c", m] = outs.tile([P, N_TILE], F32, name="new_c", tag="new_c")
+                    new_c = lasting.tile([P, N_TILE], F32, name="new_c", tag="new_c")
                     nc.vector.tensor_add(
-                        out=value["new_c", m][:], in0=value["f", m][:], in1=value["i", m][:]
+                        out=new_c[:], in0=value["f", chunk, m][:], in1=value["i", chunk, m][:]
                     )
                     nc.sync.dma_start(
-                        out=out_state[rows, HID + chunk * N_TILE : HID + (chunk + 1) * N_TILE],
-                        in_=value["new_c", m][:],
+                        out=out_state[
+                            m * P : (m + 1) * P,
+                            HID + chunk * N_TILE : HID + (chunk + 1) * N_TILE,
+                        ],
+                        in_=new_c[:],
                     )
+                    value["new_c", chunk, m] = new_c
             if gate == "o":
                 for m in row_tiles:
                     rows = slice(m * P, (m + 1) * P)
-                    new_h = outs.tile([P, N_TILE], F32, name="new_h", tag="new_h")
+                    new_h = lasting.tile([P, N_TILE], F32, name="new_h", tag="new_h")
                     nc.vector.tensor_mul(
-                        out=new_h[:], in0=value["o", m][:], in1=value["tanh_c", m][:]
+                        out=new_h[:], in0=value["o", chunk, m][:], in1=value["tanh_c", chunk, m][:]
                     )
                     nc.sync.dma_start(out=out_h[rows, cols], in_=new_h[:])
                     nc.sync.dma_start(out=out_state[rows, cols], in_=new_h[:])
 
-        for chunk in range(CHUNKS):
-            for gate_index, gate in enumerate(GATE_ORDER):
+        for gate in GATE_ORDER:
+            for chunk in range(CHUNKS):
                 banks = [
-                    psum.tile(
-                        [P, N_TILE], F32, name="sum%d" % m, tag=("even", "odd")[gate_index % 2]
-                    )
+                    psum.tile([P, N_TILE], F32, name="sum%d" % m, tag=("even", "odd")[chunk % 2])
                     for m in range(ROW_TILES)
                 ]
-                if chunk == CHUNKS - 1 and gate in GATE_ORDER[-2:]:
+                if gate == "o":
                     for m in range(ROW_TILES):
                         for matrix in MATRICES:
                             for g in range(PASSES[matrix]):
                                 mx_pass(banks[m], gate, matrix, g, chunk, m)
-                        after_gate(gate, chunk, banks, [m])
+                        after_passes(gate, chunk, banks, [m])
                 else:
                     for matrix in MATRICES:
-                        if chunk == 0 and gate_index == 0:
+                        if gate == GATE_ORDER[0] and chunk == 0:
                             for m in range(ROW_TILES):
                                 quantise_rows(matrix, m)
                         for g in range(PASSES[matrix]):
                             for m in range(ROW_TILES):
                                 mx_pass(banks[m], gate, matrix, g, chunk, m)
-                    after_gate(gate, chunk, banks, range(ROW_TILES))
+                    after_passes(gate, chunk, banks, range(ROW_TILES))

@@ -60,8 +60,8 @@ def tile_bilaterallstmcell_kernel(
         ctx.enter_context(tc.manual_schedule())
         keep = ctx.enter_context(tc.tile_pool(name="keep", bufs=1))
         stage = ctx.enter_context(tc.tile_pool(name="stage", bufs=4))
-        brief = ctx.enter_context(tc.tile_pool(name="brief", bufs=ROW_TILES))
-        lasting = ctx.enter_context(tc.tile_pool(name="lasting", bufs=ROW_TILES * CHUNKS))
+        gates = ctx.enter_context(tc.tile_pool(name="gates", bufs=ROW_TILES))
+        outs = ctx.enter_context(tc.tile_pool(name="outs", bufs=ROW_TILES * CHUNKS))
         psum = ctx.enter_context(tc.psum_pool(name="psum", bufs=ROW_TILES))
 
         identity = keep.tile([P, P], F32, name="identity")
@@ -127,8 +127,8 @@ def tile_bilaterallstmcell_kernel(
             )
             c_prev[chunk] = tile_c
 
-        for gate in GATE_ORDER:
-            for chunk in range(CHUNKS):
+        for chunk in range(CHUNKS):
+            for gate in GATE_ORDER:
                 for matrix in MATRICES:
                     if chunk == 0:
                         if gate == GATE_ORDER[0]:
@@ -141,16 +141,26 @@ def tile_bilaterallstmcell_kernel(
         codes = {}
         code_planes = {}
 
+        sorted_words = {}
+
+        def sort_words(matrix, m):
+            passes = PASSES[matrix]
+            tidy = stage.tile([P, passes * WORDS_PASS], F32, name="tidy", tag="tidy")
+            nc.vector.tensor_copy(
+                out=tidy[:].rearrange("r (g u j) -> r g u j", g=passes, u=2),
+                in_=raw[matrix, m][:].bitcast(F32).rearrange("r (g j u) -> r g u j", g=passes, u=2),
+            )
+            sorted_words[matrix, m] = tidy
+
         def quantise_rows(matrix, m):
             passes = PASSES[matrix]
-            raw_words = raw[matrix, m][:].bitcast(F32)
             flipped = psum.tile([P, N_TILE], F32, name="flipped", tag="odd")
             for g in range(passes):
                 for u in range(2):
                     slot = 2 * g + u
                     nc.tensor.transpose(
                         out=flipped[:, slot * P : (slot + 1) * P],
-                        in_=raw_words[:, WORDS_PASS * g + u : WORDS_PASS * (g + 1) : 2],
+                        in_=sorted_words[matrix, m][:, slot * P : (slot + 1) * P],
                         identity=identity[:],
                     )
             grouped = stage.tile(
@@ -188,80 +198,72 @@ def tile_bilaterallstmcell_kernel(
 
         value = {}
 
-        def after_passes(gate, chunk, banks, row_tiles):
+        def after_gate(gate, chunk, banks, row_tiles):
             cols = slice(chunk * N_TILE, (chunk + 1) * N_TILE)
             if gate == "o":
                 for m in row_tiles:
-                    value["tanh_c", chunk, m] = brief.tile(
-                        [P, N_TILE], F32, name="tanh_c", tag="tanh_c"
-                    )
+                    value["tanh_c", m] = gates.tile([P, N_TILE], F32, name="tanh_c", tag="tanh_c")
                     nc.scalar.activation(
-                        out=value["tanh_c", chunk, m][:],
-                        in_=value["new_c", chunk, m][:],
-                        func=ACT.Tanh,
+                        out=value["tanh_c", m][:], in_=value["new_c", m][:], func=ACT.Tanh
                     )
             for m in row_tiles:
-                pool = lasting if gate == "i" else brief
-                value[gate, chunk, m] = pool.tile([P, N_TILE], F32, name="gate_" + gate, tag=gate)
+                value[gate, m] = gates.tile([P, N_TILE], F32, name="gate_" + gate, tag=gate)
                 nc.scalar.activation(
-                    out=value[gate, chunk, m][:],
+                    out=value[gate, m][:],
                     in_=banks[m][:],
                     func=(ACT.Tanh if gate == "c" else ACT.Sigmoid),
                 )
             if gate == "c":
                 for m in row_tiles:
                     nc.vector.tensor_mul(
-                        out=value["i", chunk, m][:],
-                        in0=value["i", chunk, m][:],
-                        in1=value["c", chunk, m][:],
+                        out=value["i", m][:], in0=value["i", m][:], in1=value["c", m][:]
                     )
             if gate == "f":
                 for m in row_tiles:
+                    rows = slice(m * P, (m + 1) * P)
                     nc.vector.tensor_mul(
-                        out=value["f", chunk, m][:],
-                        in0=value["f", chunk, m][:],
-                        in1=c_prev[chunk][:, m, :],
+                        out=value["f", m][:], in0=value["f", m][:], in1=c_prev[chunk][:, m, :]
                     )
-                    new_c = lasting.tile([P, N_TILE], F32, name="new_c", tag="new_c")
+                    value["new_c", m] = outs.tile([P, N_TILE], F32, name="new_c", tag="new_c")
                     nc.vector.tensor_add(
-                        out=new_c[:], in0=value["f", chunk, m][:], in1=value["i", chunk, m][:]
+                        out=value["new_c", m][:], in0=value["f", m][:], in1=value["i", m][:]
                     )
                     nc.sync.dma_start(
-                        out=out_state[
-                            m * P : (m + 1) * P,
-                            HID + chunk * N_TILE : HID + (chunk + 1) * N_TILE,
-                        ],
-                        in_=new_c[:],
+                        out=out_state[rows, HID + chunk * N_TILE : HID + (chunk + 1) * N_TILE],
+                        in_=value["new_c", m][:],
                     )
-                    value["new_c", chunk, m] = new_c
             if gate == "o":
                 for m in row_tiles:
                     rows = slice(m * P, (m + 1) * P)
-                    new_h = lasting.tile([P, N_TILE], F32, name="new_h", tag="new_h")
+                    new_h = outs.tile([P, N_TILE], F32, name="new_h", tag="new_h")
                     nc.vector.tensor_mul(
-                        out=new_h[:], in0=value["o", chunk, m][:], in1=value["tanh_c", chunk, m][:]
+                        out=new_h[:], in0=value["o", m][:], in1=value["tanh_c", m][:]
                     )
                     nc.sync.dma_start(out=out_h[rows, cols], in_=new_h[:])
                     nc.sync.dma_start(out=out_state[rows, cols], in_=new_h[:])
 
-        for gate in GATE_ORDER:
-            for chunk in range(CHUNKS):
+        for chunk in range(CHUNKS):
+            for gate_index, gate in enumerate(GATE_ORDER):
                 banks = [
-                    psum.tile([P, N_TILE], F32, name="sum%d" % m, tag=("even", "odd")[chunk % 2])
+                    psum.tile(
+                        [P, N_TILE], F32, name="sum%d" % m, tag=("even", "odd")[gate_index % 2]
+                    )
                     for m in range(ROW_TILES)
                 ]
-                if gate == "o":
+                if chunk == CHUNKS - 1 and gate in GATE_ORDER[-2:]:
                     for m in range(ROW_TILES):
                         for matrix in MATRICES:
                             for g in range(PASSES[matrix]):
                                 mx_pass(banks[m], gate, matrix, g, chunk, m)
-                        after_passes(gate, chunk, banks, [m])
+                        after_gate(gate, chunk, banks, [m])
                 else:
                     for matrix in MATRICES:
-                        if gate == GATE_ORDER[0] and chunk == 0:
+                        if chunk == 0 and gate_index == 0:
+                            for m in range(ROW_TILES):
+                                sort_words(matrix, m)
                             for m in range(ROW_TILES):
                                 quantise_rows(matrix, m)
-                        for g in range(PASSES[matrix]):
-                            for m in range(ROW_TILES):
+                        for m in range(ROW_TILES):
+                            for g in range(PASSES[matrix]):
                                 mx_pass(banks[m], gate, matrix, g, chunk, m)
-                    after_passes(gate, chunk, banks, range(ROW_TILES))
+                    after_gate(gate, chunk, banks, range(ROW_TILES))

@@ -95,9 +95,10 @@ def tile_bilaterallstmcell_kernel(
             for quadrant in range(QUADRANTS):
                 first = 32 * quadrant
                 rows = slice(LIVE_ROWS * quadrant, LIVE_ROWS * (quadrant + 1))
-                nc.sync.dma_start(
-                    out=plane[first : first + LIVE_ROWS * passes, :].bitcast(I32),
-                    in_=dram_scales[gate, matrix][:, rows, :].bitcast(I32),
+                queue, word = (nc.gpsimd, F32) if gate in GATE_ORDER[-2:] else (nc.sync, I32)
+                queue.dma_start(
+                    out=plane[first : first + LIVE_ROWS * passes, :].bitcast(word),
+                    in_=dram_scales[gate, matrix][:, rows, :].bitcast(word),
                 )
 
         def load_words(gate, matrix, chunk):

@@ -89,7 +89,7 @@ def tile_bilaterallstmcell_kernel(
                 nc.sync.dma_start(out=rows[:], in_=operand[matrix][m * P : (m + 1) * P, :])
                 raw[matrix, m] = rows
 
-        def load_scales(gate, matrix):
+        def load_scales(gate, matrix, cols):
             passes = PASSES[matrix]
             plane = weight_planes[gate, matrix]
             for quadrant in range(QUADRANTS):
@@ -97,8 +97,8 @@ def tile_bilaterallstmcell_kernel(
                 rows = slice(LIVE_ROWS * quadrant, LIVE_ROWS * (quadrant + 1))
                 queue, word = (nc.gpsimd, F32) if gate in GATE_ORDER[-2:] else (nc.sync, I32)
                 queue.dma_start(
-                    out=plane[first : first + LIVE_ROWS * passes, :].bitcast(word),
-                    in_=dram_scales[gate, matrix][:, rows, :].bitcast(word),
+                    out=plane[first : first + LIVE_ROWS * passes, cols].bitcast(word),
+                    in_=dram_scales[gate, matrix][:, rows, cols].bitcast(word),
                 )
 
         def load_words(gate, matrix, chunk):
@@ -131,10 +131,13 @@ def tile_bilaterallstmcell_kernel(
         for chunk in range(CHUNKS):
             for gate in GATE_ORDER:
                 for matrix in MATRICES:
-                    if chunk == 0:
-                        if gate == GATE_ORDER[0]:
-                            load_operand(matrix)
-                        load_scales(gate, matrix)
+                    if chunk == 0 and gate == GATE_ORDER[0]:
+                        load_operand(matrix)
+                    if gate in GATE_ORDER[-2:]:
+                        if chunk == 0:
+                            load_scales(gate, matrix, slice(0, HID))
+                    else:
+                        load_scales(gate, matrix, slice(chunk * N_TILE, (chunk + 1) * N_TILE))
                     load_words(gate, matrix, chunk)
                 if gate == "f":
                     load_c_prev(chunk)

@@ -246,6 +246,21 @@ def tile_bilaterallstmcell_kernel(
                     nc.sync.dma_start(out=out_h[rows, cols], in_=new_h[:])
                     nc.sync.dma_start(out=out_state[rows, cols], in_=new_h[:])
 
+        def after_last_pass(chunk, bank, m):
+            rows = slice(m * P, (m + 1) * P)
+            tanh_c = gates.tile([P, N_TILE], F32, name="tanh_c", tag="tanh_c")
+            nc.scalar.activation(out=tanh_c[:], in_=value["new_c", m][:], func=ACT.Tanh)
+            gate_o = gates.tile([P, N_TILE], F32, name="gate_o", tag="o")
+            new_h = outs.tile([P, N_TILE], F32, name="new_h", tag="new_h")
+            half = N_TILE // 2
+            for first in (0, half):
+                here = slice(first, first + half)
+                cols = slice(chunk * N_TILE + first, chunk * N_TILE + first + half)
+                nc.scalar.activation(out=gate_o[:, here], in_=bank[:, here], func=ACT.Sigmoid)
+                nc.vector.tensor_mul(out=new_h[:, here], in0=gate_o[:, here], in1=tanh_c[:, here])
+                nc.sync.dma_start(out=out_h[rows, cols], in_=new_h[:, here])
+                nc.sync.dma_start(out=out_state[rows, cols], in_=new_h[:, here])
+
         for chunk in range(CHUNKS):
             for gate_index, gate in enumerate(GATE_ORDER):
                 banks = [
@@ -259,7 +274,10 @@ def tile_bilaterallstmcell_kernel(
                         for matrix in MATRICES:
                             for g in range(PASSES[matrix]):
                                 mx_pass(banks[m], gate, matrix, g, chunk, m)
-                        after_gate(gate, chunk, banks, [m])
+                        if gate == GATE_ORDER[-1] and m == ROW_TILES - 1:
+                            after_last_pass(chunk, banks[m], m)
+                        else:
+                            after_gate(gate, chunk, banks, [m])
                 else:
                     for matrix in MATRICES:
                         if chunk == 0 and gate_index == 0:

from contextlib import ExitStack

import concourse.mybir as mybir
from concourse.masks import make_identity

F32 = mybir.dt.float32
BF16 = mybir.dt.bfloat16
I32 = mybir.dt.int32
U32 = mybir.dt.uint32
U8 = mybir.dt.uint8
FP8X4 = mybir.dt.float8_e4m3fn_x4
ACT = mybir.ActivationFunctionType

P = 128
PACK = 4
K_PASS = P * PACK
WORDS_PASS = K_PASS // 2
QUADRANTS = 4
LIVE_ROWS = 4

BATCH, D_IN, HID = 512, 512, 1024
ROW_TILES = BATCH // P
N_TILE = 512
CHUNKS = HID // N_TILE

GATES_AS_GIVEN = "ifoc"
GATE_ORDER = "icfo"
MATRICES = "WUV"
PASSES = {"W": D_IN // K_PASS, "U": HID // K_PASS, "V": HID // K_PASS}

K_TOTAL = D_IN + 2 * HID
FLOPS = 2 * BATCH * K_TOTAL * 4 * HID
BYTES = (
    2 * BATCH * (D_IN + 3 * HID)
    + K_TOTAL * 4 * HID
    + K_TOTAL * 4 * HID // 32
    + 4 * BATCH * 3 * HID
)


def tile_bilaterallstmcell_kernel(
    tc, x, hidden_memory_tm1, hidden_memory_tm2, *weights_and_outputs
):
    nc = tc.nc
    out_h, out_state = weights_and_outputs[24:]
    dram_words = {}
    dram_scales = {}
    for gate_index, gate in enumerate(GATES_AS_GIVEN):
        for matrix_index, matrix in enumerate(MATRICES):
            first = 2 * (len(MATRICES) * gate_index + matrix_index)
            dram_words[gate, matrix] = weights_and_outputs[first]
            dram_scales[gate, matrix] = weights_and_outputs[first + 1]
    operand = {
        "W": x,
        "U": hidden_memory_tm1[:, 0:HID],
        "V": hidden_memory_tm2[:, 0:HID],
    }

    with ExitStack() as ctx:
        ctx.enter_context(tc.manual_schedule())
        keep = ctx.enter_context(tc.tile_pool(name="keep", bufs=1))
        stage = ctx.enter_context(tc.tile_pool(name="stage", bufs=4))
        gates = ctx.enter_context(tc.tile_pool(name="gates", bufs=ROW_TILES))
        outs = ctx.enter_context(tc.tile_pool(name="outs", bufs=ROW_TILES * CHUNKS))
        psum = ctx.enter_context(tc.psum_pool(name="psum", bufs=ROW_TILES))

        identity = keep.tile([P, P], F32, name="identity")
        make_identity(nc, identity[:])
        warm = keep.tile([P, 1], F32, name="warm")
        nc.vector.memset(warm[:], 0.0)
        nc.scalar.activation(out=warm[:], in_=warm[:], func=ACT.Sigmoid)

        weight_planes = {}
        for gate in GATE_ORDER:
            for matrix in MATRICES:
                plane = keep.tile(
                    [P, HID], U8, name="plane_%s%s" % (matrix, gate), align_bytes=64
                )
                nc.vector.memset(plane[:].bitcast(I32), 0)
                weight_planes[gate, matrix] = plane

        raw = {}
        weight_words = {}

        def load_operand(matrix):
            width = PASSES[matrix] * K_PASS
            for m in range(ROW_TILES):
                rows = keep.tile([P, width], BF16, name="raw_%s%d" % (matrix, m))
                nc.sync.dma_start(out=rows[:], in_=operand[matrix][m * P : (m + 1) * P, :])
                raw[matrix, m] = rows

        def load_scales(gate, matrix, cols):
            passes = PASSES[matrix]
            plane = weight_planes[gate, matrix]
            for quadrant in range(QUADRANTS):
                first = 32 * quadrant
                rows = slice(LIVE_ROWS * quadrant, LIVE_ROWS * (quadrant + 1))
                queue, word = (nc.gpsimd, F32) if gate in GATE_ORDER[-2:] else (nc.sync, I32)
                queue.dma_start(
                    out=plane[first : first + LIVE_ROWS * passes, cols].bitcast(word),
                    in_=dram_scales[gate, matrix][:, rows, cols].bitcast(word),
                )

        def load_words(gate, matrix, chunk):
            words = keep.tile(
                [P, PASSES[matrix], N_TILE],
                U32,
                name="words_%s%s_%d" % (matrix, gate, chunk),
                align_bytes=64,
            )
            source = dram_words[gate, matrix].rearrange("g p n t -> p g (n t)").bitcast(I32)
            nc.sync.dma_start(
                out=words[:].bitcast(I32),
                in_=source[:, :, chunk * N_TILE : (chunk + 1) * N_TILE],
            )
            weight_words[gate, matrix, chunk] = words

        c_prev = {}

        def load_c_prev(chunk):
            first = HID + chunk * N_TILE
            tile_c = keep.tile([P, ROW_TILES, N_TILE], BF16, name="c_prev%d" % chunk)
            nc.sync.dma_start(
                out=tile_c[:],
                in_=hidden_memory_tm1[:, first : first + N_TILE].rearrange(
                    "(m p) n -> p m n", p=P
                ),
            )
            c_prev[chunk] = tile_c

        for chunk in range(CHUNKS):
            for gate in GATE_ORDER:
                for matrix in MATRICES:
                    if chunk == 0 and gate == GATE_ORDER[0]:
                        load_operand(matrix)
                    if gate in GATE_ORDER[-2:]:
                        if chunk == 0:
                            load_scales(gate, matrix, slice(0, HID))
                    else:
                        load_scales(gate, matrix, slice(chunk * N_TILE, (chunk + 1) * N_TILE))
                    load_words(gate, matrix, chunk)
                if gate == "f":
                    load_c_prev(chunk)

        codes = {}
        code_planes = {}

        sorted_words = {}

        def sort_words(matrix, m):
            passes = PASSES[matrix]
            tidy = stage.tile([P, passes * WORDS_PASS], F32, name="tidy", tag="tidy")
            nc.vector.tensor_copy(
                out=tidy[:].rearrange("r (g u j) -> r g u j", g=passes, u=2),
                in_=raw[matrix, m][:].bitcast(F32).rearrange("r (g j u) -> r g u j", g=passes, u=2),
            )
            sorted_words[matrix, m] = tidy

        def quantise_rows(matrix, m):
            passes = PASSES[matrix]
            flipped = psum.tile([P, N_TILE], F32, name="flipped", tag="odd")
            for g in range(passes):
                for u in range(2):
                    slot = 2 * g + u
                    nc.tensor.transpose(
                        out=flipped[:, slot * P : (slot + 1) * P],
                        in_=sorted_words[matrix, m][:, slot * P : (slot + 1) * P],
                        identity=identity[:],
                    )
            grouped = stage.tile(
                [P, passes * P * PACK], BF16, name="grouped", tag="grouped", align_bytes=64
            )
            nc.scalar.copy(
                out=grouped[:].bitcast(F32).rearrange("p (g r u) -> p g r u", g=passes, u=2),
                in_=flipped[:, 0 : passes * 2 * P].rearrange(
                    "p (g u r) -> p g r u", g=passes, u=2
                ),
            )
            packed = keep.tile(
                [P, passes * P], U32, name="codes_%s%d" % (matrix, m), align_bytes=64
            )
            plane = keep.tile(
                [P, passes * P], U8, name="code_plane_%s%d" % (matrix, m), align_bytes=64
            )
            nc.vector.quantize_mx(out=packed[:].bitcast(FP8X4), scales=plane[:], in_=grouped[:])
            codes[matrix, m] = packed
            code_planes[matrix, m] = plane

        def mx_pass(bank, gate, matrix, g, chunk, m):
            rows = slice(g * P, (g + 1) * P)
            nc.tensor.matmul_mx(
                out=bank[:],
                lhsT=codes[matrix, m][:, rows].bitcast(FP8X4),
                lhsT_scale=code_planes[matrix, m][:, rows],
                rhs=weight_words[gate, matrix, chunk][:, g, :].bitcast(FP8X4),
                rhs_scale=weight_planes[gate, matrix][
                    LIVE_ROWS * g : P, chunk * N_TILE : (chunk + 1) * N_TILE
                ],
                start=(matrix == MATRICES[0]),
                stop=(matrix == MATRICES[-1] and g == PASSES[matrix] - 1),
            )

        value = {}

        def after_gate(gate, chunk, banks, row_tiles):
            cols = slice(chunk * N_TILE, (chunk + 1) * N_TILE)
            if gate == "o":
                for m in row_tiles:
                    value["tanh_c", m] = gates.tile([P, N_TILE], F32, name="tanh_c", tag="tanh_c")
                    nc.scalar.activation(
                        out=value["tanh_c", m][:], in_=value["new_c", m][:], func=ACT.Tanh
                    )
            for m in row_tiles:
                value[gate, m] = gates.tile([P, N_TILE], F32, name="gate_" + gate, tag=gate)
                nc.scalar.activation(
                    out=value[gate, m][:],
                    in_=banks[m][:],
                    func=(ACT.Tanh if gate == "c" else ACT.Sigmoid),
                )
            if gate == "c":
                for m in row_tiles:
                    nc.vector.tensor_mul(
                        out=value["i", m][:], in0=value["i", m][:], in1=value["c", m][:]
                    )
            if gate == "f":
                for m in row_tiles:
                    rows = slice(m * P, (m + 1) * P)
                    nc.vector.tensor_mul(
                        out=value["f", m][:], in0=value["f", m][:], in1=c_prev[chunk][:, m, :]
                    )
                    value["new_c", m] = outs.tile([P, N_TILE], F32, name="new_c", tag="new_c")
                    nc.vector.tensor_add(
                        out=value["new_c", m][:], in0=value["f", m][:], in1=value["i", m][:]
                    )
                    nc.sync.dma_start(
                        out=out_state[rows, HID + chunk * N_TILE : HID + (chunk + 1) * N_TILE],
                        in_=value["new_c", m][:],
                    )
            if gate == "o":
                for m in row_tiles:
                    rows = slice(m * P, (m + 1) * P)
                    new_h = outs.tile([P, N_TILE], F32, name="new_h", tag="new_h")
                    nc.vector.tensor_mul(
                        out=new_h[:], in0=value["o", m][:], in1=value["tanh_c", m][:]
                    )
                    nc.sync.dma_start(out=out_h[rows, cols], in_=new_h[:])
                    nc.sync.dma_start(out=out_state[rows, cols], in_=new_h[:])

        def after_last_pass(chunk, bank, m):
            rows = slice(m * P, (m + 1) * P)
            tanh_c = gates.tile([P, N_TILE], F32, name="tanh_c", tag="tanh_c")
            nc.scalar.activation(out=tanh_c[:], in_=value["new_c", m][:], func=ACT.Tanh)
            gate_o = gates.tile([P, N_TILE], F32, name="gate_o", tag="o")
            new_h = outs.tile([P, N_TILE], F32, name="new_h", tag="new_h")
            half = N_TILE // 2
            for first in (0, half):
                here = slice(first, first + half)
                cols = slice(chunk * N_TILE + first, chunk * N_TILE + first + half)
                nc.scalar.activation(out=gate_o[:, here], in_=bank[:, here], func=ACT.Sigmoid)
                nc.vector.tensor_mul(out=new_h[:, here], in0=gate_o[:, here], in1=tanh_c[:, here])
                nc.sync.dma_start(out=out_h[rows, cols], in_=new_h[:, here])
                nc.sync.dma_start(out=out_state[rows, cols], in_=new_h[:, here])

        for chunk in range(CHUNKS):
            for gate_index, gate in enumerate(GATE_ORDER):
                banks = [
                    psum.tile(
                        [P, N_TILE], F32, name="sum%d" % m, tag=("even", "odd")[gate_index % 2]
                    )
                    for m in range(ROW_TILES)
                ]
                if chunk == CHUNKS - 1 and gate in GATE_ORDER[-2:]:
                    for m in range(ROW_TILES):
                        for matrix in MATRICES:
                            for g in range(PASSES[matrix]):
                                mx_pass(banks[m], gate, matrix, g, chunk, m)
                        if gate == GATE_ORDER[-1] and m == ROW_TILES - 1:
                            after_last_pass(chunk, banks[m], m)
                        else:
                            after_gate(gate, chunk, banks, [m])
                else:
                    for matrix in MATRICES:
                        if chunk == 0 and gate_index == 0:
                            for m in range(ROW_TILES):
                                sort_words(matrix, m)
                            for m in range(ROW_TILES):
                                quantise_rows(matrix, m)
                        for m in range(ROW_TILES):
                            for g in range(PASSES[matrix]):
                                mx_pass(banks[m], gate, matrix, g, chunk, m)
                    after_gate(gate, chunk, banks, range(ROW_TILES))
